import numpy as np
import ml_dtypes


def mxq(x, axis, fmt="e4m3"):
    dtype, down = {"e4m3": (ml_dtypes.float8_e4m3fn, 7), "e5m2": (ml_dtypes.float8_e5m2, 14)}[fmt]
    v = np.moveaxis(np.asarray(x, np.float32).astype(ml_dtypes.bfloat16).astype(np.float64), axis, -1)
    blocks = v.reshape(v.shape[:-1] + (-1, 32))
    amax = np.abs(blocks).max(-1, keepdims=True)
    byte = np.maximum(np.where(amax > 0, np.frexp(amax)[1] - 1 + 127, 0) - down, 1)
    scale = np.exp2(byte - 127.0)
    codes = (blocks / scale).astype(np.float32).astype(dtype).astype(np.float64)
    return np.moveaxis((codes * scale).reshape(v.shape), -1, axis)


WIDE = False


def mx_kscale(k):
    if not WIDE:
        return np.ones(k)
    levels = np.array([30, -30])
    if k % 512:
        return np.exp2(np.random.permutation(np.resize(levels, k // 32))).repeat(32)
    a = np.empty((k // 512, 16))
    for p in range(k // 512):
        a[p, :8] = np.random.permutation(np.resize(levels, 8))
        for g in range(8):
            far = levels[np.abs(levels - a[p, g]) >= 10]
            a[p, g + 8] = far[np.random.randint(len(far))]
    return np.exp2(a.ravel()).repeat(32)


BF16 = ml_dtypes.bfloat16


def bf(x):
    return np.asarray(x, np.float32).astype(BF16)


def f64(x):
    return np.asarray(x).astype(np.float64)


B, L, D, H = 1, 1024, 512, 8
LN_EPS = 1e-5


def setup_inputs():
    s = mx_kscale(H * D)
    return {"heads": bf(np.random.standard_normal((H, L, D)) * 0.25 * s.reshape(H, D)[:, None, :]),
            "q": bf(np.random.standard_normal((B, L, D))),
            "proj_w": bf(np.random.standard_normal((D, H * D)) * 4.0 / np.sqrt(H * D) / s[None, :]),
            "proj_b": bf(np.random.standard_normal(D) * 0.1),
            "ln_gamma": bf(1.0 + np.random.standard_normal(D) * 0.1),
            "ln_beta": bf(np.random.standard_normal(D) * 0.1)}


def reference(heads, q, proj_w, proj_b, ln_gamma, ln_beta):
    hc = f64(heads).transpose(1, 0, 2).reshape(B, L, H * D)
    o = (mxq(hc, 2, "e5m2") @ mxq(f64(proj_w), 1, "e5m2").T) + f64(proj_b)
    x = o + f64(q)
    mu = x.mean(-1, keepdims=True)
    var = ((x - mu) ** 2).mean(-1, keepdims=True)
    return (x - mu) / np.sqrt(var + LN_EPS) * f64(ln_gamma) + f64(ln_beta)

@@ -1,0 +1,246 @@
+from contextlib import ExitStack
+
+import concourse.mybir as mybir
+from concourse.masks import make_identity
+
+L, D, H = 1024, 512, 8
+LN_EPS = 1e-5
+FLOPS = 2 * L * D * H * D
+
+F32 = mybir.dt.float32
+BF16 = mybir.dt.bfloat16
+I32 = mybir.dt.int32
+U32 = mybir.dt.uint32
+U8 = mybir.dt.uint8
+FP8X4 = mybir.dt.float8_e5m2_x4
+ALU = mybir.AluOpType
+ACT = mybir.ActivationFunctionType
+
+P = 128
+SLABS = 4
+WORDS = D // 2
+TILES = L // P
+FIRST = 4
+PAIRS = H + (TILES - FIRST)
+CHUNKS = 2 * PAIRS
+PRESORTED = tuple(c for c in range(2, 19) if c % 5 != 0)
+Q_AFTER = (5, 11)
+ON_SCALAR = ()
+SLOTS = {18: (0, 1), 19: (2,), 20: (3,), 21: (4,), 22: (5,)}
+QB_STEP = (7, 8, 9, 10, 13, 14, 15, 16)
+
+
+def tile_multiheadattention_pb_kernel(tc, heads, q, proj_w, proj_b, ln_gamma, ln_beta, out):
+    nc = tc.nc
+    with ExitStack() as ctx:
+        keep = ctx.enter_context(tc.tile_pool(name="keep", bufs=1))
+        ring = ctx.enter_context(tc.tile_pool(name="ring", bufs=4))
+        banks = ctx.enter_context(tc.psum_pool(name="banks", bufs=4))
+        ctx.enter_context(tc.manual_schedule())
+
+        def chunk_source(c):
+            pair, second = divmod(c, 2)
+            if pair < H and not second:
+                return proj_w[:, pair * D:(pair + 1) * D].rearrange("(a p) k -> p a k", p=P)
+            if pair < H:
+                return heads[pair, 0:FIRST * P, :].rearrange("(p a) k -> p a k", a=SLABS)
+            t = FIRST + pair - H
+            return heads[second * SLABS:(second + 1) * SLABS, t * P:(t + 1) * P, :].rearrange("a p k -> p a k")
+
+        def token_rows(x, t):
+            if t < FIRST:
+                return x[0, 0:FIRST * P, :].rearrange("(p a) d -> p a d", a=SLABS)[:, t, :]
+            return x[0, t * P:(t + 1) * P, :]
+
+        vec_rows = keep.tile([P, D], BF16, name="vec_rows")
+        nc.vector.memset(vec_rows[:].bitcast(I32), 0)
+        for r, vec in enumerate((proj_b, ln_gamma, ln_beta)):
+            nc.scalar.dma_start(out=vec_rows[r:r + 1, :], in_=vec.rearrange("(o d) -> o d", o=1))
+        ident_bf = keep.tile([P, P], BF16, name="ident_bf")
+        make_identity(nc, ident_bf[:])
+        ident = keep.tile([P, P], F32, name="ident")
+        make_identity(nc, ident[:])
+        eps = keep.tile([P, 1], F32, name="eps")
+        nc.vector.memset(eps[:], 0.0)
+        nc.vector.tensor_scalar(out=eps[:], in0=eps[:], scalar1=LN_EPS, scalar2=None, op0=ALU.add)
+
+        raw = []
+        q_sb = keep.tile([P, TILES, D], BF16, name="q_sb")
+        for c in range(CHUNKS):
+            tile = keep.tile([P, SLABS, D], BF16, name="raw%d" % c, align_bytes=64)
+            raw.append(tile)
+            src = chunk_source(c)
+            if c < 2:
+                nc.sync.dma_start(out=tile[:, 0:2, :], in_=src[:, 0:2, :])
+                nc.sync.dma_start(out=tile[:, 2:4, :], in_=src[:, 2:4, :])
+            else:
+                nc.sync.dma_start(out=tile[:], in_=src)
+            if c == Q_AFTER[0]:
+                nc.sync.dma_start(out=q_sb[:, 0:FIRST, :], in_=q[0, 0:FIRST * P, :].rearrange("(p a) d -> p a d", a=SLABS))
+            if c == Q_AFTER[1]:
+                nc.sync.dma_start(out=q_sb[:, FIRST:TILES, :], in_=q[0, FIRST * P:L, :].rearrange("(a p) d -> p a d", p=P))
+
+        spread = keep.tile([P, 3, D], F32, name="spread")
+
+        def spread_vectors():
+            for r in range(3):
+                ps = banks.tile([P, D], F32, name="acc", tag="acc")
+                nc.tensor.matmul(ps[:], lhsT=ident_bf[:, r:r + 1].to_broadcast([P, P]), rhs=vec_rows[:], start=True, stop=True)
+                nc.scalar.activation(out=spread[:, r, :], in_=ps[:], func=ACT.Copy)
+
+        bias, gamma, beta = spread[:, 0, :], spread[:, 1, :], spread[:, 2, :]
+
+        x = keep.tile([P, TILES, D], F32, name="x")
+        res = keep.tile([P, TILES, D], F32, name="res")
+        squares = keep.tile([P, D], F32, name="squares")
+        total = keep.tile([P, TILES, 8], F32, name="total")
+        mean = keep.tile([P, TILES, 8], F32, name="mean")
+        sumsq = keep.tile([P, TILES, 8], F32, name="sumsq")
+        rstd = keep.tile([P, TILES, 8], F32, name="rstd")
+
+        sorted_words, grouped, codes, scales, acc = {}, {}, {}, {}, {}
+
+        def raw_words(c):
+            return raw[c][:].rearrange("p a k -> p (a k)").bitcast(F32)
+
+        def presort(c):
+            if c not in PRESORTED:
+                return
+            tile = ring.tile([P, SLABS, 2, P], F32, name="sorted", tag="sorted", align_bytes=64)
+            src = raw_words(c).rearrange("p (a w u) -> p a u w", a=SLABS, u=2)
+            if c in ON_SCALAR:
+                nc.scalar.copy(out=tile[:], in_=src)
+            else:
+                nc.vector.tensor_copy(out=tile[:], in_=src)
+            sorted_words[c] = tile
+
+        def transpose(c):
+            grouped[c] = ring.tile([P, SLABS * D], BF16, name="grouped", tag="grouped", align_bytes=64)
+            target = grouped[c][:].bitcast(F32)
+            for half in range(2):
+                ps = banks.tile([P, 2, 2, P], F32, name="turned", tag="turned")
+                for i in range(2):
+                    a = 2 * half + i
+                    for u in range(2):
+                        if c in PRESORTED:
+                            src = sorted_words[c][:, a, u, :]
+                        else:
+                            src = raw_words(c)[:, a * WORDS + u:(a + 1) * WORDS:2]
+                        nc.tensor.transpose(ps[:, i, u, :], src, ident[:])
+                nc.scalar.copy(
+                    out=target[:, half * D:(half + 1) * D].rearrange("p (i r u) -> p i r u", i=2, u=2),
+                    in_=ps[:].rearrange("p i u r -> p i r u"),
+                )
+
+        def quantize(c):
+            if c < 2 * H and c % 2 == 0:
+                codes[c] = keep.tile([P, D], U32, name="w_codes%d" % c, align_bytes=64)
+                scales[c] = keep.tile([P, D], U8, name="w_scales%d" % c, align_bytes=64)
+            else:
+                codes[c] = ring.tile([P, D], U32, name="h_codes", tag="h_codes", align_bytes=64)
+                scales[c] = ring.tile([P, D], U8, name="h_scales", tag="h_scales", align_bytes=64)
+            nc.vector.quantize_mx(out=codes[c][:].bitcast(FP8X4), scales=scales[c][:], in_=grouped[c][:])
+
+        def mx_pass(t, h, c, a, part, parts):
+            width = D // parts
+            if h == 0:
+                acc[t, part] = banks.tile([P, width], F32, name="acc", tag="acc")
+            tokens = slice(a * P, (a + 1) * P)
+            cols = slice(part * width, (part + 1) * width)
+            nc.tensor.matmul_mx(
+                out=acc[t, part][:],
+                lhsT=codes[c][:, tokens].bitcast(FP8X4),
+                lhsT_scale=scales[c][:, tokens],
+                rhs=codes[2 * h][:, cols].bitcast(FP8X4),
+                rhs_scale=scales[2 * h][:, cols],
+                start=(h == 0),
+                stop=(h == H - 1),
+            )
+
+        def multiply(pair, parts=1):
+            if pair < H:
+                for t in range(FIRST):
+                    mx_pass(t, pair, 2 * pair + 1, t, 0, 1)
+            else:
+                for part in range(parts):
+                    for h in range(H):
+                        mx_pass(FIRST + pair - H, h, 2 * pair + h // SLABS, h % SLABS, part, parts)
+
+        def residual(t):
+            nc.vector.tensor_tensor(out=x[:, t, :], in0=q_sb[:, t, :], in1=bias, op=ALU.add)
+
+        def drain(t, part=0, parts=1):
+            cols = slice(part * D // parts, (part + 1) * D // parts)
+            nc.vector.scalar_tensor_tensor(
+                out=x[:, t, cols], in0=acc[t, part][:], scalar=1.0, in1=x[:, t, cols], op0=ALU.mult, op1=ALU.add,
+                accum_out=total[:, t, part:part + 1],
+            )
+
+        def mean_of(t, parts=1):
+            if parts == 1:
+                nc.vector.tensor_scalar(out=mean[:, t, 0:1], in0=total[:, t, 0:1], scalar1=1.0 / D, scalar2=None, op0=ALU.mult)
+            else:
+                nc.vector.tensor_scalar(
+                    out=mean[:, t, 0:1], in0=total[:, t, 0:1], scalar1=total[:, t, 1:2], scalar2=1.0 / D, op0=ALU.add, op1=ALU.mult,
+                )
+
+        def deviation(t):
+            nc.scalar.activation(
+                out=squares[:], in_=x[:, t, :], func=ACT.Square, scale=-1.0, bias=mean[:, t, 0:1],
+                accum_out=sumsq[:, t, 0:1],
+            )
+            nc.scalar.activation(
+                out=rstd[:, t, 0:1], in_=sumsq[:, t, 0:1], func=ACT.Abs_reciprocal_sqrt, scale=1.0 / D, bias=eps[:],
+            )
+
+        def centre(t):
+            nc.vector.scalar_tensor_tensor(
+                out=res[:, t, :], in0=x[:, t, :], scalar=mean[:, t, 0:1], in1=gamma, op0=ALU.subtract, op1=ALU.mult,
+            )
+
+        def finish(t, parts=1):
+            for part in range(parts):
+                cols = slice(part * D // parts, (part + 1) * D // parts)
+                nc.vector.scalar_tensor_tensor(
+                    out=res[:, t, cols], in0=res[:, t, cols], scalar=rstd[:, t, 0:1], in1=beta[:, cols], op0=ALU.mult, op1=ALU.add,
+                )
+                nc.sync.dma_start(out=token_rows(out, t)[:, cols], in_=res[:, t, cols])
+
+        def norm_slot(k):
+            if k < TILES - 1:
+                drain(k)
+            if k >= 1:
+                deviation(k - 1)
+                centre(k - 1)
+            if k < TILES - 1:
+                mean_of(k)
+            if k >= 2:
+                finish(k - 2)
+
+        spread_vectors()
+        presort(0)
+        presort(1)
+        for c in range(CHUNKS):
+            transpose(c)
+            if c >= 1:
+                quantize(c - 1)
+            if c + 2 < CHUNKS:
+                presort(c + 2)
+            if c in QB_STEP:
+                residual(QB_STEP.index(c))
+            for k in SLOTS.get(c, ()):
+                norm_slot(k)
+            if c >= 3 and c % 2 == 1:
+                multiply((c - 3) // 2)
+        last = TILES - 1
+        quantize(CHUNKS - 1)
+        norm_slot(last - 1)
+        multiply(PAIRS - 1, parts=2)
+        norm_slot(last)
+        drain(last, 0, 2)
+        finish(last - 1)
+        drain(last, 1, 2)
+        mean_of(last, parts=2)
+        deviation(last)
+        centre(last)
+        finish(last, parts=2)

@@ -23,10 +23,16 @@ TILES = L // P
 FIRST = 4
 PAIRS = H + (TILES - FIRST)
 CHUNKS = 2 * PAIRS
-PRESORTED = tuple(c for c in range(2, 19) if c % 5 != 0)
+PRESORTED = tuple(range(4, 21, 2))
 Q_AFTER = (5, 11)
 ON_SCALAR = ()
-SLOTS = {18: (0, 1), 19: (2,), 20: (3,), 21: (4,), 22: (5,)}
+WARM = 0
+RATE = 2
+SLOT_FIRST = 1
+LOOK = 2
+OPEN = 3
+RAW_BUFS = 16
+ACC_BANKS = 3
 QB_STEP = (7, 8, 9, 10, 13, 14, 15, 16)
 
 
@@ -35,7 +41,7 @@ def tile_multiheadattention_pb_kernel(tc, heads, q, proj_w, proj_b, ln_gamma, ln
     with ExitStack() as ctx:
         keep = ctx.enter_context(tc.tile_pool(name="keep", bufs=1))
         ring = ctx.enter_context(tc.tile_pool(name="ring", bufs=4))
-        banks = ctx.enter_context(tc.psum_pool(name="banks", bufs=4))
+        banks = ctx.enter_context(tc.psum_pool(name="banks", bufs=1))
         ctx.enter_context(tc.manual_schedule())
 
         def chunk_source(c):
@@ -53,13 +59,13 @@ def tile_multiheadattention_pb_kernel(tc, heads, q, proj_w, proj_b, ln_gamma, ln
             return x[0, t * P:(t + 1) * P, :]
 
         vec_rows = keep.tile([P, D], BF16, name="vec_rows")
-        nc.vector.memset(vec_rows[:].bitcast(I32), 0)
+        nc.gpsimd.memset(vec_rows[:].bitcast(I32), 0)
         for r, vec in enumerate((proj_b, ln_gamma, ln_beta)):
-            nc.scalar.dma_start(out=vec_rows[r:r + 1, :], in_=vec.rearrange("(o d) -> o d", o=1))
-        ident_bf = keep.tile([P, P], BF16, name="ident_bf")
-        make_identity(nc, ident_bf[:])
+            nc.sync.dma_start(out=vec_rows[r:r + 1, :], in_=vec.rearrange("(o d) -> o d", o=1))
         ident = keep.tile([P, P], F32, name="ident")
         make_identity(nc, ident[:])
+        pick = keep.tile([P, 4], BF16, name="pick")
+        nc.vector.tensor_copy(out=pick[:], in_=ident[:, 0:4])
         eps = keep.tile([P, 1], F32, name="eps")
         nc.vector.memset(eps[:], 0.0)
         nc.vector.tensor_scalar(out=eps[:], in0=eps[:], scalar1=LN_EPS, scalar2=None, op0=ALU.add)
@@ -67,7 +73,7 @@ def tile_multiheadattention_pb_kernel(tc, heads, q, proj_w, proj_b, ln_gamma, ln
         raw = []
         q_sb = keep.tile([P, TILES, D], BF16, name="q_sb")
         for c in range(CHUNKS):
-            tile = keep.tile([P, SLABS, D], BF16, name="raw%d" % c, align_bytes=64)
+            tile = ring.tile([P, SLABS, D], BF16, name="raw", tag="raw", bufs=RAW_BUFS, align_bytes=64)
             raw.append(tile)
             src = chunk_source(c)
             if c < 2:
@@ -84,21 +90,20 @@ def tile_multiheadattention_pb_kernel(tc, heads, q, proj_w, proj_b, ln_gamma, ln
 
         def spread_vectors():
             for r in range(3):
-                ps = banks.tile([P, D], F32, name="acc", tag="acc")
-                nc.tensor.matmul(ps[:], lhsT=ident_bf[:, r:r + 1].to_broadcast([P, P]), rhs=vec_rows[:], start=True, stop=True)
+                ps = banks.tile([P, D], F32, name="acc", tag="acc", bufs=ACC_BANKS)
+                nc.tensor.matmul(ps[:], lhsT=pick[:, r:r + 1].to_broadcast([P, P]), rhs=vec_rows[:], start=True, stop=True)
                 nc.scalar.activation(out=spread[:, r, :], in_=ps[:], func=ACT.Copy)
 
         bias, gamma, beta = spread[:, 0, :], spread[:, 1, :], spread[:, 2, :]
 
         x = keep.tile([P, TILES, D], F32, name="x")
-        res = keep.tile([P, TILES, D], F32, name="res")
         squares = keep.tile([P, D], F32, name="squares")
         total = keep.tile([P, TILES, 8], F32, name="total")
         mean = keep.tile([P, TILES, 8], F32, name="mean")
         sumsq = keep.tile([P, TILES, 8], F32, name="sumsq")
         rstd = keep.tile([P, TILES, 8], F32, name="rstd")
 
-        sorted_words, grouped, codes, scales, acc = {}, {}, {}, {}, {}
+        sorted_words, grouped, codes, scales, acc, res = {}, {}, {}, {}, {}, {}
 
         def raw_words(c):
             return raw[c][:].rearrange("p a k -> p (a k)").bitcast(F32)
@@ -118,7 +123,7 @@ def tile_multiheadattention_pb_kernel(tc, heads, q, proj_w, proj_b, ln_gamma, ln
             grouped[c] = ring.tile([P, SLABS * D], BF16, name="grouped", tag="grouped", align_bytes=64)
             target = grouped[c][:].bitcast(F32)
             for half in range(2):
-                ps = banks.tile([P, 2, 2, P], F32, name="turned", tag="turned")
+                ps = banks.tile([P, 2, 2, P], F32, name="turned", tag="turned", bufs=8 - ACC_BANKS)
                 for i in range(2):
                     a = 2 * half + i
                     for u in range(2):
@@ -133,18 +138,14 @@ def tile_multiheadattention_pb_kernel(tc, heads, q, proj_w, proj_b, ln_gamma, ln
                 )
 
         def quantize(c):
-            if c < 2 * H and c % 2 == 0:
-                codes[c] = keep.tile([P, D], U32, name="w_codes%d" % c, align_bytes=64)
-                scales[c] = keep.tile([P, D], U8, name="w_scales%d" % c, align_bytes=64)
-            else:
-                codes[c] = ring.tile([P, D], U32, name="h_codes", tag="h_codes", align_bytes=64)
-                scales[c] = ring.tile([P, D], U8, name="h_scales", tag="h_scales", align_bytes=64)
+            codes[c] = keep.tile([P, D], U32, name="codes%d" % c, align_bytes=64)
+            scales[c] = keep.tile([P, D], U8, name="scales%d" % c, align_bytes=64)
             nc.vector.quantize_mx(out=codes[c][:].bitcast(FP8X4), scales=scales[c][:], in_=grouped[c][:])
 
         def mx_pass(t, h, c, a, part, parts):
             width = D // parts
             if h == 0:
-                acc[t, part] = banks.tile([P, width], F32, name="acc", tag="acc")
+                acc[t, part] = banks.tile([P, width], F32, name="acc", tag="acc", bufs=ACC_BANKS)
             tokens = slice(a * P, (a + 1) * P)
             cols = slice(part * width, (part + 1) * width)
             nc.tensor.matmul_mx(
@@ -157,14 +158,17 @@ def tile_multiheadattention_pb_kernel(tc, heads, q, proj_w, proj_b, ln_gamma, ln
                 stop=(h == H - 1),
             )
 
-        def multiply(pair, parts=1):
-            if pair < H:
-                for t in range(FIRST):
-                    mx_pass(t, pair, 2 * pair + 1, t, 0, 1)
-            else:
-                for part in range(parts):
-                    for h in range(H):
-                        mx_pass(FIRST + pair - H, h, 2 * pair + h // SLABS, h % SLABS, part, parts)
+        def multiply_pass(h):
+            for t in range(OPEN):
+                mx_pass(t, h, 2 * h + 1, t, 0, 1)
+
+        def multiply_tile(t, parts=1):
+            for part in range(parts):
+                for h in range(H):
+                    if t < FIRST:
+                        mx_pass(t, h, 2 * h + 1, t, part, parts)
+                    else:
+                        mx_pass(t, h, 2 * (H + t - FIRST) + h // SLABS, h % SLABS, part, parts)
 
         def residual(t):
             nc.vector.tensor_tensor(out=x[:, t, :], in0=q_sb[:, t, :], in1=bias, op=ALU.add)
@@ -189,58 +193,82 @@ def tile_multiheadattention_pb_kernel(tc, heads, q, proj_w, proj_b, ln_gamma, ln
                 out=squares[:], in_=x[:, t, :], func=ACT.Square, scale=-1.0, bias=mean[:, t, 0:1],
                 accum_out=sumsq[:, t, 0:1],
             )
+
+        def inverse_std(t):
             nc.scalar.activation(
                 out=rstd[:, t, 0:1], in_=sumsq[:, t, 0:1], func=ACT.Abs_reciprocal_sqrt, scale=1.0 / D, bias=eps[:],
             )
 
         def centre(t):
+            res[t] = ring.tile([P, D], F32, name="res", tag="res")
             nc.vector.scalar_tensor_tensor(
-                out=res[:, t, :], in0=x[:, t, :], scalar=mean[:, t, 0:1], in1=gamma, op0=ALU.subtract, op1=ALU.mult,
+                out=res[t][:], in0=x[:, t, :], scalar=mean[:, t, 0:1], in1=gamma, op0=ALU.subtract, op1=ALU.mult,
             )
 
         def finish(t, parts=1):
             for part in range(parts):
                 cols = slice(part * D // parts, (part + 1) * D // parts)
                 nc.vector.scalar_tensor_tensor(
-                    out=res[:, t, cols], in0=res[:, t, cols], scalar=rstd[:, t, 0:1], in1=beta[:, cols], op0=ALU.mult, op1=ALU.add,
+                    out=res[t][:, cols], in0=res[t][:, cols], scalar=rstd[:, t, 0:1], in1=beta[:, cols], op0=ALU.mult, op1=ALU.add,
                 )
-                nc.sync.dma_start(out=token_rows(out, t)[:, cols], in_=res[:, t, cols])
+                nc.sync.dma_start(out=token_rows(out, t)[:, cols], in_=res[t][:, cols])
 
-        def norm_slot(k):
-            if k < TILES - 1:
-                drain(k)
-            if k >= 1:
-                deviation(k - 1)
-                centre(k - 1)
-            if k < TILES - 1:
-                mean_of(k)
-            if k >= 2:
-                finish(k - 2)
-
-        spread_vectors()
-        presort(0)
-        presort(1)
-        for c in range(CHUNKS):
-            transpose(c)
-            if c >= 1:
-                quantize(c - 1)
-            if c + 2 < CHUNKS:
-                presort(c + 2)
-            if c in QB_STEP:
-                residual(QB_STEP.index(c))
-            for k in SLOTS.get(c, ()):
-                norm_slot(k)
-            if c >= 3 and c % 2 == 1:
-                multiply((c - 3) // 2)
         last = TILES - 1
-        quantize(CHUNKS - 1)
-        norm_slot(last - 1)
-        multiply(PAIRS - 1, parts=2)
-        norm_slot(last)
+        queue = []
+        for t in range(last):
+            queue.append((drain, t))
+            if t >= 1:
+                queue.extend([(inverse_std, t - 1), (centre, t - 1)])
+            queue.extend([(mean_of, t), (deviation, t)])
+            if t >= 1:
+                queue.append((finish, t - 1))
+        closed = []
+
+        def norm_steps(budget):
+            while queue and budget > 0:
+                step, t = queue[0]
+                if step is drain and t not in closed:
+                    return
+                queue.pop(0)
+                step(t)
+                if step in (drain, finish, centre):
+                    budget -= 1
+
+        if WARM:
+            nc.scalar.activation(out=squares[:, 0:1], in_=eps[:], func=ACT.Abs_reciprocal_sqrt)
+        spread_vectors()
+        for c in range(LOOK):
+            presort(c)
+        for r in range(H + TILES - OPEN + 1):
+            for c in (2 * r, 2 * r + 1):
+                if c < CHUNKS:
+                    if SLOT_FIRST:
+                        norm_steps(RATE)
+                    transpose(c)
+                if 1 <= c <= CHUNKS:
+                    quantize(c - 1)
+                if c + LOOK < CHUNKS:
+                    presort(c + LOOK)
+                if c in QB_STEP:
+                    residual(QB_STEP.index(c))
+                if not SLOT_FIRST or c >= CHUNKS:
+                    norm_steps(RATE)
+            if 1 <= r <= H:
+                multiply_pass(r - 1)
+                if r == H:
+                    closed.extend(range(OPEN))
+            elif r > H:
+                t = OPEN + r - H - 1
+                multiply_tile(t, parts=2 if t == last else 1)
+                closed.append(t)
+        norm_steps(len(queue))
         drain(last, 0, 2)
-        finish(last - 1)
+        inverse_std(last - 1)
+        centre(last - 1)
         drain(last, 1, 2)
         mean_of(last, parts=2)
         deviation(last)
+        finish(last - 1)
         centre(last)
+        inverse_std(last)
         finish(last, parts=2)

@@ -23,15 +23,20 @@ TILES = L // P
 FIRST = 4
 PAIRS = H + (TILES - FIRST)
 CHUNKS = 2 * PAIRS
-PRESORTED = tuple(range(4, 21, 2))
+PRESORTED = tuple(range(4, 19, 2))
 Q_AFTER = (5, 11)
 ON_SCALAR = ()
 WARM = 0
-RATE = 2
-SLOT_FIRST = 1
+RATE = 3
+SLOT_FIRST = 0
 LOOK = 2
 OPEN = 3
-RAW_BUFS = 16
+RAW_BUFS = 10
+SINGLE_W = 8
+QPAIR = 0
+ORDER = 1
+RES_GROUP = 1
+MEAN_S = 1
 ACC_BANKS = 3
 QB_STEP = (7, 8, 9, 10, 13, 14, 15, 16)
 
@@ -44,19 +49,39 @@ def tile_multiheadattention_pb_kernel(tc, heads, q, proj_w, proj_b, ln_gamma, ln
         banks = ctx.enter_context(tc.psum_pool(name="banks", bufs=1))
         ctx.enter_context(tc.manual_schedule())
 
-        def chunk_source(c):
+        def load_chunk(c):
             pair, second = divmod(c, 2)
             if pair < H and not second:
-                return proj_w[:, pair * D:(pair + 1) * D].rearrange("(a p) k -> p a k", p=P)
-            if pair < H:
-                return heads[pair, 0:FIRST * P, :].rearrange("(p a) k -> p a k", a=SLABS)
-            t = FIRST + pair - H
-            return heads[second * SLABS:(second + 1) * SLABS, t * P:(t + 1) * P, :].rearrange("a p k -> p a k")
+                span = 1 if pair < SINGLE_W else 2
+                if span == 2 and pair % 2 == 1:
+                    return
+                tile = keep.tile([P, SLABS, span * D], BF16, name="w_raw%d" % pair, align_bytes=64)
+                src = proj_w[:, pair * D:(pair + span) * D].rearrange("(a p) k -> p a k", p=P)
+                for i in range(span):
+                    raw[c + 2 * i] = tile[:].bitcast(F32)[:, :, i * WORDS:(i + 1) * WORDS]
+                dst = tile[:]
+            else:
+                tile = ring.tile([P, SLABS, D], BF16, name="h_raw", tag="h_raw", bufs=RAW_BUFS, align_bytes=64)
+                raw[c] = tile[:].bitcast(F32)
+                if pair < H:
+                    src = heads[pair, 0:FIRST * P, :].rearrange("(p a) k -> p a k", a=SLABS)
+                    dst = tile[:]
+                else:
+                    duo, step = divmod(c - 2 * H, SLABS)
+                    rows = slice((FIRST + 2 * duo) * P, (FIRST + 2 * duo + 2) * P)
+                    src = heads[2 * step:2 * step + 2, rows, :].rearrange("h (p j) k -> p h (j k)", j=2)
+                    dst = tile[:].rearrange("p (h j) k -> p h (j k)", j=2)
+            if c < 2:
+                nc.sync.dma_start(out=dst[:, 0:2, :], in_=src[:, 0:2, :])
+                nc.sync.dma_start(out=dst[:, 2:4, :], in_=src[:, 2:4, :])
+            else:
+                nc.sync.dma_start(out=dst, in_=src)
 
         def token_rows(x, t):
             if t < FIRST:
                 return x[0, 0:FIRST * P, :].rearrange("(p a) d -> p a d", a=SLABS)[:, t, :]
-            return x[0, t * P:(t + 1) * P, :]
+            first = t - t % 2
+            return x[0, first * P:(first + 2) * P, :].rearrange("(p j) d -> p j d", j=2)[:, t % 2, :]
 
         vec_rows = keep.tile([P, D], BF16, name="vec_rows")
         nc.gpsimd.memset(vec_rows[:].bitcast(I32), 0)
@@ -70,21 +95,17 @@ def tile_multiheadattention_pb_kernel(tc, heads, q, proj_w, proj_b, ln_gamma, ln
         nc.vector.memset(eps[:], 0.0)
         nc.vector.tensor_scalar(out=eps[:], in0=eps[:], scalar1=LN_EPS, scalar2=None, op0=ALU.add)
 
-        raw = []
+        raw = {}
         q_sb = keep.tile([P, TILES, D], BF16, name="q_sb")
         for c in range(CHUNKS):
-            tile = ring.tile([P, SLABS, D], BF16, name="raw", tag="raw", bufs=RAW_BUFS, align_bytes=64)
-            raw.append(tile)
-            src = chunk_source(c)
-            if c < 2:
-                nc.sync.dma_start(out=tile[:, 0:2, :], in_=src[:, 0:2, :])
-                nc.sync.dma_start(out=tile[:, 2:4, :], in_=src[:, 2:4, :])
-            else:
-                nc.sync.dma_start(out=tile[:], in_=src)
+            load_chunk(c)
             if c == Q_AFTER[0]:
                 nc.sync.dma_start(out=q_sb[:, 0:FIRST, :], in_=q[0, 0:FIRST * P, :].rearrange("(p a) d -> p a d", a=SLABS))
             if c == Q_AFTER[1]:
-                nc.sync.dma_start(out=q_sb[:, FIRST:TILES, :], in_=q[0, FIRST * P:L, :].rearrange("(a p) d -> p a d", p=P))
+                nc.sync.dma_start(
+                    out=q_sb[:, FIRST:TILES, :].rearrange("p (g j) d -> p g (j d)", j=2),
+                    in_=q[0, FIRST * P:L, :].rearrange("(g p j) d -> p g (j d)", p=P, j=2),
+                )
 
         spread = keep.tile([P, 3, D], F32, name="spread")
 
@@ -94,7 +115,7 @@ def tile_multiheadattention_pb_kernel(tc, heads, q, proj_w, proj_b, ln_gamma, ln
                 nc.tensor.matmul(ps[:], lhsT=pick[:, r:r + 1].to_broadcast([P, P]), rhs=vec_rows[:], start=True, stop=True)
                 nc.scalar.activation(out=spread[:, r, :], in_=ps[:], func=ACT.Copy)
 
-        bias, gamma, beta = spread[:, 0, :], spread[:, 1, :], spread[:, 2, :]
+        gamma, beta = spread[:, 1, :], spread[:, 2, :]
 
         x = keep.tile([P, TILES, D], F32, name="x")
         squares = keep.tile([P, D], F32, name="squares")
@@ -104,15 +125,13 @@ def tile_multiheadattention_pb_kernel(tc, heads, q, proj_w, proj_b, ln_gamma, ln
         rstd = keep.tile([P, TILES, 8], F32, name="rstd")
 
         sorted_words, grouped, codes, scales, acc, res = {}, {}, {}, {}, {}, {}
-
-        def raw_words(c):
-            return raw[c][:].rearrange("p a k -> p (a k)").bitcast(F32)
+        pair_codes, pair_scales = {}, {}
 
         def presort(c):
             if c not in PRESORTED:
                 return
             tile = ring.tile([P, SLABS, 2, P], F32, name="sorted", tag="sorted", align_bytes=64)
-            src = raw_words(c).rearrange("p (a w u) -> p a u w", a=SLABS, u=2)
+            src = raw[c].rearrange("p a (w u) -> p a u w", u=2)
             if c in ON_SCALAR:
                 nc.scalar.copy(out=tile[:], in_=src)
             else:
@@ -120,8 +139,10 @@ def tile_multiheadattention_pb_kernel(tc, heads, q, proj_w, proj_b, ln_gamma, ln
             sorted_words[c] = tile
 
         def transpose(c):
-            grouped[c] = ring.tile([P, SLABS * D], BF16, name="grouped", tag="grouped", align_bytes=64)
-            target = grouped[c][:].bitcast(F32)
+            if c % 2 == 0:
+                both = ring.tile([P, 2 * SLABS * D], BF16, name="grouped", tag="grouped", bufs=3, align_bytes=64)
+                grouped[c // 2] = both
+            target = grouped[c // 2][:, (c % 2) * SLABS * D:(c % 2 + 1) * SLABS * D].bitcast(F32)
             for half in range(2):
                 ps = banks.tile([P, 2, 2, P], F32, name="turned", tag="turned", bufs=8 - ACC_BANKS)
                 for i in range(2):
@@ -130,7 +151,7 @@ def tile_multiheadattention_pb_kernel(tc, heads, q, proj_w, proj_b, ln_gamma, ln
                         if c in PRESORTED:
                             src = sorted_words[c][:, a, u, :]
                         else:
-                            src = raw_words(c)[:, a * WORDS + u:(a + 1) * WORDS:2]
+                            src = raw[c][:, a, u:WORDS:2]
                         nc.tensor.transpose(ps[:, i, u, :], src, ident[:])
                 nc.scalar.copy(
                     out=target[:, half * D:(half + 1) * D].rearrange("p (i r u) -> p i r u", i=2, u=2),
@@ -138,9 +159,22 @@ def tile_multiheadattention_pb_kernel(tc, heads, q, proj_w, proj_b, ln_gamma, ln
                 )
 
         def quantize(c):
-            codes[c] = keep.tile([P, D], U32, name="codes%d" % c, align_bytes=64)
-            scales[c] = keep.tile([P, D], U8, name="scales%d" % c, align_bytes=64)
-            nc.vector.quantize_mx(out=codes[c][:].bitcast(FP8X4), scales=scales[c][:], in_=grouped[c][:])
+            pair, second = divmod(c, 2)
+            joint = QPAIR and pair < PAIRS - 1
+            if joint and not second:
+                return
+            if joint or not second:
+                pair_codes[pair] = keep.tile([P, 2 * D], U32, name="codes%d" % pair, align_bytes=64)
+                pair_scales[pair] = keep.tile([P, 2 * D], U8, name="scales%d" % pair, align_bytes=64)
+                for i in range(2):
+                    codes[2 * pair + i] = pair_codes[pair][:, i * D:(i + 1) * D]
+                    scales[2 * pair + i] = pair_scales[pair][:, i * D:(i + 1) * D]
+            first, end = (0, 2) if joint else (second, second + 1)
+            nc.vector.quantize_mx(
+                out=pair_codes[pair][:, first * D:end * D].bitcast(FP8X4),
+                scales=pair_scales[pair][:, first * D:end * D],
+                in_=grouped[pair][:, first * SLABS * D:end * SLABS * D],
+            )
 
         def mx_pass(t, h, c, a, part, parts):
             width = D // parts
@@ -168,10 +202,12 @@ def tile_multiheadattention_pb_kernel(tc, heads, q, proj_w, proj_b, ln_gamma, ln
                     if t < FIRST:
                         mx_pass(t, h, 2 * h + 1, t, part, parts)
                     else:
-                        mx_pass(t, h, 2 * (H + t - FIRST) + h // SLABS, h % SLABS, part, parts)
+                        mx_pass(t, h, 2 * H + SLABS * ((t - FIRST) // 2) + h // 2, 2 * (h % 2) + t % 2, part, parts)
 
-        def residual(t):
-            nc.vector.tensor_tensor(out=x[:, t, :], in0=q_sb[:, t, :], in1=bias, op=ALU.add)
+        def residual(g):
+            tiles = slice(g * RES_GROUP, (g + 1) * RES_GROUP)
+            wide = spread[:, 0:1, :].to_broadcast([P, RES_GROUP, D])
+            nc.vector.tensor_tensor(out=x[:, tiles, :], in0=q_sb[:, tiles, :], in1=wide, op=ALU.add)
 
         def drain(t, part=0, parts=1):
             cols = slice(part * D // parts, (part + 1) * D // parts)
@@ -181,7 +217,9 @@ def tile_multiheadattention_pb_kernel(tc, heads, q, proj_w, proj_b, ln_gamma, ln
             )
 
         def mean_of(t, parts=1):
-            if parts == 1:
+            if parts == 1 and MEAN_S:
+                nc.scalar.activation(out=mean[:, t, 0:1], in_=total[:, t, 0:1], func=ACT.Copy, scale=1.0 / D)
+            elif parts == 1:
                 nc.vector.tensor_scalar(out=mean[:, t, 0:1], in0=total[:, t, 0:1], scalar1=1.0 / D, scalar2=None, op0=ALU.mult)
             else:
                 nc.vector.tensor_scalar(
@@ -216,12 +254,21 @@ def tile_multiheadattention_pb_kernel(tc, heads, q, proj_w, proj_b, ln_gamma, ln
         last = TILES - 1
         queue = []
         for t in range(last):
-            queue.append((drain, t))
-            if t >= 1:
-                queue.extend([(inverse_std, t - 1), (centre, t - 1)])
-            queue.extend([(mean_of, t), (deviation, t)])
-            if t >= 1:
-                queue.append((finish, t - 1))
+            if ORDER == 0:
+                queue.append((drain, t))
+                if t >= 1:
+                    queue.extend([(inverse_std, t - 1), (centre, t - 1)])
+                queue.append((mean_of, t))
+                if t >= 1:
+                    queue.append((finish, t - 1))
+                queue.append((deviation, t))
+            else:
+                if t >= 1:
+                    queue.extend([(centre, t - 1), (inverse_std, t - 1)])
+                queue.extend([(drain, t), (mean_of, t)])
+                if t >= 1:
+                    queue.append((finish, t - 1))
+                queue.append((deviation, t))
         closed = []
 
         def norm_steps(budget):

@@ -18,27 +18,19 @@ ACT = mybir.ActivationFunctionType
 
 P = 128
 SLABS = 4
-WORDS = D // 2
+PAIRS = D // 2
 TILES = L // P
-FIRST = 4
-PAIRS = H + (TILES - FIRST)
-CHUNKS = 2 * PAIRS
-PRESORTED = tuple(range(4, 19, 2))
-Q_AFTER = (5, 11)
-ON_SCALAR = ()
-WARM = 0
-RATE = 3
-SLOT_FIRST = 0
-LOOK = 2
+EARLY = SLABS
+CHUNKS = 2 * H + 2 * (TILES - EARLY)
+LAST = TILES - 1
+STAT = 8
+
 OPEN = 3
-RAW_BUFS = 10
-SINGLE_W = 8
-QPAIR = 0
-ORDER = 1
-RES_GROUP = 1
-MEAN_S = 1
-ACC_BANKS = 3
-QB_STEP = (7, 8, 9, 10, 13, 14, 15, 16)
+SUM_BANKS = OPEN
+Q_AFTER = (5, 11)
+SORTED_ROUNDS = range(2, 10)
+AHEAD = 2
+NORM_RATE = 3
 
 
 def tile_multiheadattention_pb_kernel(tc, heads, q, proj_w, proj_b, ln_gamma, ln_beta, out):
@@ -49,44 +41,11 @@ def tile_multiheadattention_pb_kernel(tc, heads, q, proj_w, proj_b, ln_gamma, ln
         banks = ctx.enter_context(tc.psum_pool(name="banks", bufs=1))
         ctx.enter_context(tc.manual_schedule())
 
-        def load_chunk(c):
-            pair, second = divmod(c, 2)
-            if pair < H and not second:
-                span = 1 if pair < SINGLE_W else 2
-                if span == 2 and pair % 2 == 1:
-                    return
-                tile = keep.tile([P, SLABS, span * D], BF16, name="w_raw%d" % pair, align_bytes=64)
-                src = proj_w[:, pair * D:(pair + span) * D].rearrange("(a p) k -> p a k", p=P)
-                for i in range(span):
-                    raw[c + 2 * i] = tile[:].bitcast(F32)[:, :, i * WORDS:(i + 1) * WORDS]
-                dst = tile[:]
-            else:
-                tile = ring.tile([P, SLABS, D], BF16, name="h_raw", tag="h_raw", bufs=RAW_BUFS, align_bytes=64)
-                raw[c] = tile[:].bitcast(F32)
-                if pair < H:
-                    src = heads[pair, 0:FIRST * P, :].rearrange("(p a) k -> p a k", a=SLABS)
-                    dst = tile[:]
-                else:
-                    duo, step = divmod(c - 2 * H, SLABS)
-                    rows = slice((FIRST + 2 * duo) * P, (FIRST + 2 * duo + 2) * P)
-                    src = heads[2 * step:2 * step + 2, rows, :].rearrange("h (p j) k -> p h (j k)", j=2)
-                    dst = tile[:].rearrange("p (h j) k -> p h (j k)", j=2)
-            if c < 2:
-                nc.sync.dma_start(out=dst[:, 0:2, :], in_=src[:, 0:2, :])
-                nc.sync.dma_start(out=dst[:, 2:4, :], in_=src[:, 2:4, :])
-            else:
-                nc.sync.dma_start(out=dst, in_=src)
-
-        def token_rows(x, t):
-            if t < FIRST:
-                return x[0, 0:FIRST * P, :].rearrange("(p a) d -> p a d", a=SLABS)[:, t, :]
-            first = t - t % 2
-            return x[0, first * P:(first + 2) * P, :].rearrange("(p j) d -> p j d", j=2)[:, t % 2, :]
-
+        vectors = (proj_b, ln_gamma, ln_beta)
         vec_rows = keep.tile([P, D], BF16, name="vec_rows")
         nc.gpsimd.memset(vec_rows[:].bitcast(I32), 0)
-        for r, vec in enumerate((proj_b, ln_gamma, ln_beta)):
-            nc.sync.dma_start(out=vec_rows[r:r + 1, :], in_=vec.rearrange("(o d) -> o d", o=1))
+        for v, vec in enumerate(vectors):
+            nc.sync.dma_start(out=vec_rows[v:v + 1, :], in_=vec.rearrange("(o d) -> o d", o=1))
         ident = keep.tile([P, P], F32, name="ident")
         make_identity(nc, ident[:])
         pick = keep.tile([P, 4], BF16, name="pick")
@@ -97,134 +56,139 @@ def tile_multiheadattention_pb_kernel(tc, heads, q, proj_w, proj_b, ln_gamma, ln
 
         raw = {}
         q_sb = keep.tile([P, TILES, D], BF16, name="q_sb")
+
+        def load(c, dst, src):
+            if c < 2:
+                nc.sync.dma_start(out=dst[:, 0:2, :], in_=src[:, 0:2, :])
+                nc.sync.dma_start(out=dst[:, 2:4, :], in_=src[:, 2:4, :])
+            else:
+                nc.sync.dma_start(out=dst, in_=src)
+
+        def load_weights(c):
+            h = c // 2
+            tile = keep.tile([P, SLABS, D], BF16, name="w_raw%d" % h, align_bytes=64)
+            raw[c] = tile[:].bitcast(F32)
+            load(c, tile[:], proj_w[:, h * D:(h + 1) * D].rearrange("(a p) k -> p a k", p=P))
+
+        def load_heads(c):
+            tile = ring.tile([P, SLABS, D], BF16, name="h_raw", tag="h_raw", bufs=10, align_bytes=64)
+            raw[c] = tile[:].bitcast(F32)
+            if c < 2 * H:
+                load(c, tile[:], heads[c // 2, 0:EARLY * P, :].rearrange("(p a) k -> p a k", a=SLABS))
+            else:
+                couple, place = divmod(c - 2 * H, H // 2)
+                first, h = EARLY + 2 * couple, 2 * place
+                src = heads[h:h + 2, first * P:(first + 2) * P, :]
+                load(c, tile[:].rearrange("p (i j) k -> p i (j k)", j=2), src.rearrange("i (p j) k -> p i (j k)", j=2))
+
+        def token_rows(t):
+            if t < EARLY:
+                return out[0, 0:EARLY * P, :].rearrange("(p a) d -> p a d", a=SLABS)[:, t, :]
+            first = t - t % 2
+            return out[0, first * P:(first + 2) * P, :].rearrange("(p j) d -> p j d", j=2)[:, t % 2, :]
+
         for c in range(CHUNKS):
-            load_chunk(c)
+            if c >= 2 * H or c % 2 == 1:
+                load_heads(c)
+            else:
+                load_weights(c)
             if c == Q_AFTER[0]:
-                nc.sync.dma_start(out=q_sb[:, 0:FIRST, :], in_=q[0, 0:FIRST * P, :].rearrange("(p a) d -> p a d", a=SLABS))
+                nc.sync.dma_start(
+                    out=q_sb[:, 0:EARLY, :],
+                    in_=q[0, 0:EARLY * P, :].rearrange("(p a) d -> p a d", a=SLABS),
+                )
             if c == Q_AFTER[1]:
                 nc.sync.dma_start(
-                    out=q_sb[:, FIRST:TILES, :].rearrange("p (g j) d -> p g (j d)", j=2),
-                    in_=q[0, FIRST * P:L, :].rearrange("(g p j) d -> p g (j d)", p=P, j=2),
+                    out=q_sb[:, EARLY:TILES, :].rearrange("p (g j) d -> p g (j d)", j=2),
+                    in_=q[0, EARLY * P:L, :].rearrange("(g p j) d -> p g (j d)", p=P, j=2),
                 )
 
-        spread = keep.tile([P, 3, D], F32, name="spread")
-
-        def spread_vectors():
-            for r in range(3):
-                ps = banks.tile([P, D], F32, name="acc", tag="acc", bufs=ACC_BANKS)
-                nc.tensor.matmul(ps[:], lhsT=pick[:, r:r + 1].to_broadcast([P, P]), rhs=vec_rows[:], start=True, stop=True)
-                nc.scalar.activation(out=spread[:, r, :], in_=ps[:], func=ACT.Copy)
-
-        gamma, beta = spread[:, 1, :], spread[:, 2, :]
-
+        spread = keep.tile([P, len(vectors), D], F32, name="spread")
+        bias, gamma, beta = spread[:, 0, :], spread[:, 1, :], spread[:, 2, :]
         x = keep.tile([P, TILES, D], F32, name="x")
         squares = keep.tile([P, D], F32, name="squares")
-        total = keep.tile([P, TILES, 8], F32, name="total")
-        mean = keep.tile([P, TILES, 8], F32, name="mean")
-        sumsq = keep.tile([P, TILES, 8], F32, name="sumsq")
-        rstd = keep.tile([P, TILES, 8], F32, name="rstd")
+        total = keep.tile([P, TILES, STAT], F32, name="total")
+        mean = keep.tile([P, TILES, STAT], F32, name="mean")
+        sumsq = keep.tile([P, TILES, STAT], F32, name="sumsq")
+        rstd = keep.tile([P, TILES, STAT], F32, name="rstd")
 
-        sorted_words, grouped, codes, scales, acc, res = {}, {}, {}, {}, {}, {}
-        pair_codes, pair_scales = {}, {}
+        nc.scalar.activation(out=squares[:, 0:1], in_=eps[:], func=ACT.Abs_reciprocal_sqrt)
+
+        for v in range(len(vectors)):
+            copies = banks.tile([P, D], F32, name="sums", tag="sums", bufs=SUM_BANKS)
+            nc.tensor.matmul(copies[:], lhsT=pick[:, v:v + 1].to_broadcast([P, P]), rhs=vec_rows[:], start=True, stop=True)
+            nc.scalar.activation(out=spread[:, v, :], in_=copies[:], func=ACT.Copy)
+
+        ordered, grouped, codes, scales = {}, {}, {}, {}
+
+        def is_presorted(c):
+            return c % 2 == 0 and c // 2 in SORTED_ROUNDS
 
         def presort(c):
-            if c not in PRESORTED:
-                return
-            tile = ring.tile([P, SLABS, 2, P], F32, name="sorted", tag="sorted", align_bytes=64)
-            src = raw[c].rearrange("p a (w u) -> p a u w", u=2)
-            if c in ON_SCALAR:
-                nc.scalar.copy(out=tile[:], in_=src)
-            else:
-                nc.vector.tensor_copy(out=tile[:], in_=src)
-            sorted_words[c] = tile
+            ordered[c] = ring.tile([P, SLABS, 2, P], F32, name="ordered", tag="ordered", align_bytes=64)
+            nc.vector.tensor_copy(out=ordered[c][:], in_=raw[c].rearrange("p a (w u) -> p a u w", u=2))
 
         def transpose(c):
             if c % 2 == 0:
-                both = ring.tile([P, 2 * SLABS * D], BF16, name="grouped", tag="grouped", bufs=3, align_bytes=64)
-                grouped[c // 2] = both
-            target = grouped[c // 2][:, (c % 2) * SLABS * D:(c % 2 + 1) * SLABS * D].bitcast(F32)
+                both = ring.tile([P, 2, SLABS * D], BF16, name="grouped", tag="grouped", bufs=3, align_bytes=64)
+                grouped[c], grouped[c + 1] = both[:, 0, :], both[:, 1, :]
+            target = grouped[c].bitcast(F32)
             for half in range(2):
-                ps = banks.tile([P, 2, 2, P], F32, name="turned", tag="turned", bufs=8 - ACC_BANKS)
+                turned = banks.tile([P, 2, 2, P], F32, name="turned", tag="turned", bufs=8 - SUM_BANKS)
                 for i in range(2):
                     a = 2 * half + i
                     for u in range(2):
-                        if c in PRESORTED:
-                            src = sorted_words[c][:, a, u, :]
-                        else:
-                            src = raw[c][:, a, u:WORDS:2]
-                        nc.tensor.transpose(ps[:, i, u, :], src, ident[:])
+                        src = ordered[c][:, a, u, :] if is_presorted(c) else raw[c][:, a, u:PAIRS:2]
+                        nc.tensor.transpose(turned[:, i, u, :], src, ident[:])
                 nc.scalar.copy(
-                    out=target[:, half * D:(half + 1) * D].rearrange("p (i r u) -> p i r u", i=2, u=2),
-                    in_=ps[:].rearrange("p i u r -> p i r u"),
+                    out=target[:, half * D:(half + 1) * D].rearrange("p (i m u) -> p i m u", i=2, u=2),
+                    in_=turned[:].rearrange("p i u m -> p i m u"),
                 )
 
         def quantize(c):
-            pair, second = divmod(c, 2)
-            joint = QPAIR and pair < PAIRS - 1
-            if joint and not second:
-                return
-            if joint or not second:
-                pair_codes[pair] = keep.tile([P, 2 * D], U32, name="codes%d" % pair, align_bytes=64)
-                pair_scales[pair] = keep.tile([P, 2 * D], U8, name="scales%d" % pair, align_bytes=64)
+            if c % 2 == 0:
+                both_codes = keep.tile([P, 2, D], U32, name="codes%d" % c, align_bytes=64)
+                both_scales = keep.tile([P, 2, D], U8, name="scales%d" % c, align_bytes=64)
                 for i in range(2):
-                    codes[2 * pair + i] = pair_codes[pair][:, i * D:(i + 1) * D]
-                    scales[2 * pair + i] = pair_scales[pair][:, i * D:(i + 1) * D]
-            first, end = (0, 2) if joint else (second, second + 1)
-            nc.vector.quantize_mx(
-                out=pair_codes[pair][:, first * D:end * D].bitcast(FP8X4),
-                scales=pair_scales[pair][:, first * D:end * D],
-                in_=grouped[pair][:, first * SLABS * D:end * SLABS * D],
-            )
+                    codes[c + i], scales[c + i] = both_codes[:, i, :], both_scales[:, i, :]
+            nc.vector.quantize_mx(out=codes[c].bitcast(FP8X4), scales=scales[c], in_=grouped[c])
 
-        def mx_pass(t, h, c, a, part, parts):
+        sums = {}
+
+        def mx_pass(t, h, part=0, parts=1):
             width = D // parts
             if h == 0:
-                acc[t, part] = banks.tile([P, width], F32, name="acc", tag="acc", bufs=ACC_BANKS)
+                sums[t, part] = banks.tile([P, width], F32, name="sums", tag="sums", bufs=SUM_BANKS)
+            if t < EARLY:
+                c, a = 2 * h + 1, t
+            else:
+                c, a = 2 * H + (H // 2) * ((t - EARLY) // 2) + h // 2, 2 * (h % 2) + t % 2
             tokens = slice(a * P, (a + 1) * P)
-            cols = slice(part * width, (part + 1) * width)
+            features = slice(part * width, (part + 1) * width)
             nc.tensor.matmul_mx(
-                out=acc[t, part][:],
+                out=sums[t, part][:],
                 lhsT=codes[c][:, tokens].bitcast(FP8X4),
                 lhsT_scale=scales[c][:, tokens],
-                rhs=codes[2 * h][:, cols].bitcast(FP8X4),
-                rhs_scale=scales[2 * h][:, cols],
+                rhs=codes[2 * h][:, features].bitcast(FP8X4),
+                rhs_scale=scales[2 * h][:, features],
                 start=(h == 0),
                 stop=(h == H - 1),
             )
 
-        def multiply_pass(h):
-            for t in range(OPEN):
-                mx_pass(t, h, 2 * h + 1, t, 0, 1)
+        res = {}
 
-        def multiply_tile(t, parts=1):
-            for part in range(parts):
-                for h in range(H):
-                    if t < FIRST:
-                        mx_pass(t, h, 2 * h + 1, t, part, parts)
-                    else:
-                        mx_pass(t, h, 2 * H + SLABS * ((t - FIRST) // 2) + h // 2, 2 * (h % 2) + t % 2, part, parts)
-
-        def residual(g):
-            tiles = slice(g * RES_GROUP, (g + 1) * RES_GROUP)
-            wide = spread[:, 0:1, :].to_broadcast([P, RES_GROUP, D])
-            nc.vector.tensor_tensor(out=x[:, tiles, :], in0=q_sb[:, tiles, :], in1=wide, op=ALU.add)
+        def residual(t):
+            nc.vector.tensor_tensor(out=x[:, t, :], in0=q_sb[:, t, :], in1=bias, op=ALU.add)
 
         def drain(t, part=0, parts=1):
             cols = slice(part * D // parts, (part + 1) * D // parts)
             nc.vector.scalar_tensor_tensor(
-                out=x[:, t, cols], in0=acc[t, part][:], scalar=1.0, in1=x[:, t, cols], op0=ALU.mult, op1=ALU.add,
+                out=x[:, t, cols], in0=sums[t, part][:], scalar=1.0, in1=x[:, t, cols], op0=ALU.mult, op1=ALU.add,
                 accum_out=total[:, t, part:part + 1],
             )
 
-        def mean_of(t, parts=1):
-            if parts == 1 and MEAN_S:
-                nc.scalar.activation(out=mean[:, t, 0:1], in_=total[:, t, 0:1], func=ACT.Copy, scale=1.0 / D)
-            elif parts == 1:
-                nc.vector.tensor_scalar(out=mean[:, t, 0:1], in0=total[:, t, 0:1], scalar1=1.0 / D, scalar2=None, op0=ALU.mult)
-            else:
-                nc.vector.tensor_scalar(
-                    out=mean[:, t, 0:1], in0=total[:, t, 0:1], scalar1=total[:, t, 1:2], scalar2=1.0 / D, op0=ALU.add, op1=ALU.mult,
-                )
+        def mean_of(t):
+            nc.scalar.activation(out=mean[:, t, 0:1], in_=total[:, t, 0:1], func=ACT.Copy, scale=1.0 / D)
 
         def deviation(t):
             nc.scalar.activation(
@@ -247,75 +211,63 @@ def tile_multiheadattention_pb_kernel(tc, heads, q, proj_w, proj_b, ln_gamma, ln
             for part in range(parts):
                 cols = slice(part * D // parts, (part + 1) * D // parts)
                 nc.vector.scalar_tensor_tensor(
-                    out=res[t][:, cols], in0=res[t][:, cols], scalar=rstd[:, t, 0:1], in1=beta[:, cols], op0=ALU.mult, op1=ALU.add,
+                    out=res[t][:, cols], in0=res[t][:, cols], scalar=rstd[:, t, 0:1], in1=beta[:, cols],
+                    op0=ALU.mult, op1=ALU.add,
                 )
-                nc.sync.dma_start(out=token_rows(out, t)[:, cols], in_=res[t][:, cols])
+                nc.sync.dma_start(out=token_rows(t)[:, cols], in_=res[t][:, cols])
 
-        last = TILES - 1
-        queue = []
-        for t in range(last):
-            if ORDER == 0:
-                queue.append((drain, t))
-                if t >= 1:
-                    queue.extend([(inverse_std, t - 1), (centre, t - 1)])
-                queue.append((mean_of, t))
-                if t >= 1:
-                    queue.append((finish, t - 1))
-                queue.append((deviation, t))
-            else:
-                if t >= 1:
-                    queue.extend([(centre, t - 1), (inverse_std, t - 1)])
-                queue.extend([(drain, t), (mean_of, t)])
-                if t >= 1:
-                    queue.append((finish, t - 1))
-                queue.append((deviation, t))
+        pending = [(drain, 0), (mean_of, 0), (deviation, 0)]
+        for t in range(1, LAST):
+            pending.extend([(centre, t - 1), (inverse_std, t - 1), (drain, t), (mean_of, t), (finish, t - 1), (deviation, t)])
         closed = []
 
         def norm_steps(budget):
-            while queue and budget > 0:
-                step, t = queue[0]
+            while pending and budget > 0:
+                step, t = pending[0]
                 if step is drain and t not in closed:
                     return
-                queue.pop(0)
+                pending.pop(0)
                 step(t)
-                if step in (drain, finish, centre):
+                if step in (drain, centre, finish):
                     budget -= 1
 
-        if WARM:
-            nc.scalar.activation(out=squares[:, 0:1], in_=eps[:], func=ACT.Abs_reciprocal_sqrt)
-        spread_vectors()
-        for c in range(LOOK):
-            presort(c)
+        residual_at = [after + AHEAD + i for after in Q_AFTER for i in range(TILES // 2)]
+
         for r in range(H + TILES - OPEN + 1):
             for c in (2 * r, 2 * r + 1):
                 if c < CHUNKS:
-                    if SLOT_FIRST:
-                        norm_steps(RATE)
                     transpose(c)
                 if 1 <= c <= CHUNKS:
                     quantize(c - 1)
-                if c + LOOK < CHUNKS:
-                    presort(c + LOOK)
-                if c in QB_STEP:
-                    residual(QB_STEP.index(c))
-                if not SLOT_FIRST or c >= CHUNKS:
-                    norm_steps(RATE)
+                if is_presorted(c + AHEAD):
+                    presort(c + AHEAD)
+                if c in residual_at:
+                    residual(residual_at.index(c))
+                norm_steps(NORM_RATE)
             if 1 <= r <= H:
-                multiply_pass(r - 1)
+                for t in range(OPEN):
+                    mx_pass(t, r - 1)
                 if r == H:
                     closed.extend(range(OPEN))
             elif r > H:
                 t = OPEN + r - H - 1
-                multiply_tile(t, parts=2 if t == last else 1)
+                parts = 2 if t == LAST else 1
+                for part in range(parts):
+                    for h in range(H):
+                        mx_pass(t, h, part, parts)
                 closed.append(t)
-        norm_steps(len(queue))
-        drain(last, 0, 2)
-        inverse_std(last - 1)
-        centre(last - 1)
-        drain(last, 1, 2)
-        mean_of(last, parts=2)
-        deviation(last)
-        finish(last - 1)
-        centre(last)
-        inverse_std(last)
-        finish(last, parts=2)
+
+        norm_steps(len(pending))
+        drain(LAST, 0, 2)
+        inverse_std(LAST - 1)
+        centre(LAST - 1)
+        drain(LAST, 1, 2)
+        nc.vector.tensor_scalar(
+            out=mean[:, LAST, 0:1], in0=total[:, LAST, 0:1], scalar1=total[:, LAST, 1:2], scalar2=1.0 / D,
+            op0=ALU.add, op1=ALU.mult,
+        )
+        deviation(LAST)
+        finish(LAST - 1)
+        centre(LAST)
+        inverse_std(LAST)
+        finish(LAST, parts=2)

from contextlib import ExitStack

import concourse.mybir as mybir
from concourse.masks import make_identity

L, D, H = 1024, 512, 8
LN_EPS = 1e-5
FLOPS = 2 * L * D * H * D

F32 = mybir.dt.float32
BF16 = mybir.dt.bfloat16
I32 = mybir.dt.int32
U32 = mybir.dt.uint32
U8 = mybir.dt.uint8
FP8X4 = mybir.dt.float8_e5m2_x4
ALU = mybir.AluOpType
ACT = mybir.ActivationFunctionType

P = 128
SLABS = 4
PAIRS = D // 2
TILES = L // P
EARLY = SLABS
CHUNKS = 2 * H + 2 * (TILES - EARLY)
LAST = TILES - 1
STAT = 8

OPEN = 3
SUM_BANKS = OPEN
Q_AFTER = (5, 11)
SORTED_ROUNDS = range(2, 10)
AHEAD = 2
NORM_RATE = 3


def tile_multiheadattention_pb_kernel(tc, heads, q, proj_w, proj_b, ln_gamma, ln_beta, out):
    nc = tc.nc
    with ExitStack() as ctx:
        keep = ctx.enter_context(tc.tile_pool(name="keep", bufs=1))
        ring = ctx.enter_context(tc.tile_pool(name="ring", bufs=4))
        banks = ctx.enter_context(tc.psum_pool(name="banks", bufs=1))
        ctx.enter_context(tc.manual_schedule())

        vectors = (proj_b, ln_gamma, ln_beta)
        vec_rows = keep.tile([P, D], BF16, name="vec_rows")
        nc.gpsimd.memset(vec_rows[:].bitcast(I32), 0)
        for v, vec in enumerate(vectors):
            nc.sync.dma_start(out=vec_rows[v:v + 1, :], in_=vec.rearrange("(o d) -> o d", o=1))
        ident = keep.tile([P, P], F32, name="ident")
        make_identity(nc, ident[:])
        pick = keep.tile([P, 4], BF16, name="pick")
        nc.vector.tensor_copy(out=pick[:], in_=ident[:, 0:4])
        eps = keep.tile([P, 1], F32, name="eps")
        nc.vector.memset(eps[:], 0.0)
        nc.vector.tensor_scalar(out=eps[:], in0=eps[:], scalar1=LN_EPS, scalar2=None, op0=ALU.add)

        raw = {}
        q_sb = keep.tile([P, TILES, D], BF16, name="q_sb")

        def load(c, dst, src):
            if c < 2:
                nc.sync.dma_start(out=dst[:, 0:2, :], in_=src[:, 0:2, :])
                nc.sync.dma_start(out=dst[:, 2:4, :], in_=src[:, 2:4, :])
            else:
                nc.sync.dma_start(out=dst, in_=src)

        def load_weights(c):
            h = c // 2
            tile = keep.tile([P, SLABS, D], BF16, name="w_raw%d" % h, align_bytes=64)
            raw[c] = tile[:].bitcast(F32)
            load(c, tile[:], proj_w[:, h * D:(h + 1) * D].rearrange("(a p) k -> p a k", p=P))

        def load_heads(c):
            tile = ring.tile([P, SLABS, D], BF16, name="h_raw", tag="h_raw", bufs=10, align_bytes=64)
            raw[c] = tile[:].bitcast(F32)
            if c < 2 * H:
                load(c, tile[:], heads[c // 2, 0:EARLY * P, :].rearrange("(p a) k -> p a k", a=SLABS))
            else:
                couple, place = divmod(c - 2 * H, H // 2)
                first, h = EARLY + 2 * couple, 2 * place
                src = heads[h:h + 2, first * P:(first + 2) * P, :]
                load(c, tile[:].rearrange("p (i j) k -> p i (j k)", j=2), src.rearrange("i (p j) k -> p i (j k)", j=2))

        def token_rows(t):
            if t < EARLY:
                return out[0, 0:EARLY * P, :].rearrange("(p a) d -> p a d", a=SLABS)[:, t, :]
            first = t - t % 2
            return out[0, first * P:(first + 2) * P, :].rearrange("(p j) d -> p j d", j=2)[:, t % 2, :]

        for c in range(CHUNKS):
            if c >= 2 * H or c % 2 == 1:
                load_heads(c)
            else:
                load_weights(c)
            if c == Q_AFTER[0]:
                nc.sync.dma_start(
                    out=q_sb[:, 0:EARLY, :],
                    in_=q[0, 0:EARLY * P, :].rearrange("(p a) d -> p a d", a=SLABS),
                )
            if c == Q_AFTER[1]:
                nc.sync.dma_start(
                    out=q_sb[:, EARLY:TILES, :].rearrange("p (g j) d -> p g (j d)", j=2),
                    in_=q[0, EARLY * P:L, :].rearrange("(g p j) d -> p g (j d)", p=P, j=2),
                )

        spread = keep.tile([P, len(vectors), D], F32, name="spread")
        bias, gamma, beta = spread[:, 0, :], spread[:, 1, :], spread[:, 2, :]
        x = keep.tile([P, TILES, D], F32, name="x")
        squares = keep.tile([P, D], F32, name="squares")
        total = keep.tile([P, TILES, STAT], F32, name="total")
        mean = keep.tile([P, TILES, STAT], F32, name="mean")
        sumsq = keep.tile([P, TILES, STAT], F32, name="sumsq")
        rstd = keep.tile([P, TILES, STAT], F32, name="rstd")

        nc.scalar.activation(out=squares[:, 0:1], in_=eps[:], func=ACT.Abs_reciprocal_sqrt)

        for v in range(len(vectors)):
            copies = banks.tile([P, D], F32, name="sums", tag="sums", bufs=SUM_BANKS)
            nc.tensor.matmul(copies[:], lhsT=pick[:, v:v + 1].to_broadcast([P, P]), rhs=vec_rows[:], start=True, stop=True)
            nc.scalar.activation(out=spread[:, v, :], in_=copies[:], func=ACT.Copy)

        ordered, grouped, codes, scales = {}, {}, {}, {}

        def is_presorted(c):
            return c % 2 == 0 and c // 2 in SORTED_ROUNDS

        def presort(c):
            ordered[c] = ring.tile([P, SLABS, 2, P], F32, name="ordered", tag="ordered", align_bytes=64)
            nc.vector.tensor_copy(out=ordered[c][:], in_=raw[c].rearrange("p a (w u) -> p a u w", u=2))

        def transpose(c):
            if c % 2 == 0:
                both = ring.tile([P, 2, SLABS * D], BF16, name="grouped", tag="grouped", bufs=3, align_bytes=64)
                grouped[c], grouped[c + 1] = both[:, 0, :], both[:, 1, :]
            target = grouped[c].bitcast(F32)
            for half in range(2):
                turned = banks.tile([P, 2, 2, P], F32, name="turned", tag="turned", bufs=8 - SUM_BANKS)
                for i in range(2):
                    a = 2 * half + i
                    for u in range(2):
                        src = ordered[c][:, a, u, :] if is_presorted(c) else raw[c][:, a, u:PAIRS:2]
                        nc.tensor.transpose(turned[:, i, u, :], src, ident[:])
                nc.scalar.copy(
                    out=target[:, half * D:(half + 1) * D].rearrange("p (i m u) -> p i m u", i=2, u=2),
                    in_=turned[:].rearrange("p i u m -> p i m u"),
                )

        def quantize(c):
            if c % 2 == 0:
                both_codes = keep.tile([P, 2, D], U32, name="codes%d" % c, align_bytes=64)
                both_scales = keep.tile([P, 2, D], U8, name="scales%d" % c, align_bytes=64)
                for i in range(2):
                    codes[c + i], scales[c + i] = both_codes[:, i, :], both_scales[:, i, :]
            nc.vector.quantize_mx(out=codes[c].bitcast(FP8X4), scales=scales[c], in_=grouped[c])

        sums = {}

        def mx_pass(t, h, part=0, parts=1):
            width = D // parts
            if h == 0:
                sums[t, part] = banks.tile([P, width], F32, name="sums", tag="sums", bufs=SUM_BANKS)
            if t < EARLY:
                c, a = 2 * h + 1, t
            else:
                c, a = 2 * H + (H // 2) * ((t - EARLY) // 2) + h // 2, 2 * (h % 2) + t % 2
            tokens = slice(a * P, (a + 1) * P)
            features = slice(part * width, (part + 1) * width)
            nc.tensor.matmul_mx(
                out=sums[t, part][:],
                lhsT=codes[c][:, tokens].bitcast(FP8X4),
                lhsT_scale=scales[c][:, tokens],
                rhs=codes[2 * h][:, features].bitcast(FP8X4),
                rhs_scale=scales[2 * h][:, features],
                start=(h == 0),
                stop=(h == H - 1),
            )

        res = {}

        def residual(t):
            nc.vector.tensor_tensor(out=x[:, t, :], in0=q_sb[:, t, :], in1=bias, op=ALU.add)

        def drain(t, part=0, parts=1):
            cols = slice(part * D // parts, (part + 1) * D // parts)
            nc.vector.scalar_tensor_tensor(
                out=x[:, t, cols], in0=sums[t, part][:], scalar=1.0, in1=x[:, t, cols], op0=ALU.mult, op1=ALU.add,
                accum_out=total[:, t, part:part + 1],
            )

        def mean_of(t):
            nc.scalar.activation(out=mean[:, t, 0:1], in_=total[:, t, 0:1], func=ACT.Copy, scale=1.0 / D)

        def deviation(t):
            nc.scalar.activation(
                out=squares[:], in_=x[:, t, :], func=ACT.Square, scale=-1.0, bias=mean[:, t, 0:1],
                accum_out=sumsq[:, t, 0:1],
            )

        def inverse_std(t):
            nc.scalar.activation(
                out=rstd[:, t, 0:1], in_=sumsq[:, t, 0:1], func=ACT.Abs_reciprocal_sqrt, scale=1.0 / D, bias=eps[:],
            )

        def centre(t):
            res[t] = ring.tile([P, D], F32, name="res", tag="res")
            nc.vector.scalar_tensor_tensor(
                out=res[t][:], in0=x[:, t, :], scalar=mean[:, t, 0:1], in1=gamma, op0=ALU.subtract, op1=ALU.mult,
            )

        def finish(t, parts=1):
            for part in range(parts):
                cols = slice(part * D // parts, (part + 1) * D // parts)
                nc.vector.scalar_tensor_tensor(
                    out=res[t][:, cols], in0=res[t][:, cols], scalar=rstd[:, t, 0:1], in1=beta[:, cols],
                    op0=ALU.mult, op1=ALU.add,
                )
                nc.sync.dma_start(out=token_rows(t)[:, cols], in_=res[t][:, cols])

        pending = [(drain, 0), (mean_of, 0), (deviation, 0)]
        for t in range(1, LAST):
            pending.extend([(centre, t - 1), (inverse_std, t - 1), (drain, t), (mean_of, t), (finish, t - 1), (deviation, t)])
        closed = []

        def norm_steps(budget):
            while pending and budget > 0:
                step, t = pending[0]
                if step is drain and t not in closed:
                    return
                pending.pop(0)
                step(t)
                if step in (drain, centre, finish):
                    budget -= 1

        residual_at = [after + AHEAD + i for after in Q_AFTER for i in range(TILES // 2)]

        for r in range(H + TILES - OPEN + 1):
            for c in (2 * r, 2 * r + 1):
                if c < CHUNKS:
                    transpose(c)
                if 1 <= c <= CHUNKS:
                    quantize(c - 1)
                if is_presorted(c + AHEAD):
                    presort(c + AHEAD)
                if c in residual_at:
                    residual(residual_at.index(c))
                norm_steps(NORM_RATE)
            if 1 <= r <= H:
                for t in range(OPEN):
                    mx_pass(t, r - 1)
                if r == H:
                    closed.extend(range(OPEN))
            elif r > H:
                t = OPEN + r - H - 1
                parts = 2 if t == LAST else 1
                for part in range(parts):
                    for h in range(H):
                        mx_pass(t, h, part, parts)
                closed.append(t)

        norm_steps(len(pending))
        drain(LAST, 0, 2)
        inverse_std(LAST - 1)
        centre(LAST - 1)
        drain(LAST, 1, 2)
        nc.vector.tensor_scalar(
            out=mean[:, LAST, 0:1], in0=total[:, LAST, 0:1], scalar1=total[:, LAST, 1:2], scalar2=1.0 / D,
            op0=ALU.add, op1=ALU.mult,
        )
        deviation(LAST)
        finish(LAST - 1)
        centre(LAST)
        inverse_std(LAST)
        finish(LAST, parts=2)
